import numpy as np
import ml_dtypes


def mxq(x, axis, fmt="e4m3"):
    dtype, down = {"e4m3": (ml_dtypes.float8_e4m3fn, 7), "e5m2": (ml_dtypes.float8_e5m2, 14)}[fmt]
    v = np.moveaxis(np.asarray(x, np.float32).astype(ml_dtypes.bfloat16).astype(np.float64), axis, -1)
    blocks = v.reshape(v.shape[:-1] + (-1, 32))
    amax = np.abs(blocks).max(-1, keepdims=True)
    byte = np.maximum(np.where(amax > 0, np.frexp(amax)[1] - 1 + 127, 0) - down, 1)
    scale = np.exp2(byte - 127.0)
    codes = (blocks / scale).astype(np.float32).astype(dtype).astype(np.float64)
    return np.moveaxis((codes * scale).reshape(v.shape), -1, axis)


WIDE = False


def mx_kscale(k):
    if not WIDE:
        return np.ones(k)
    levels = np.array([10, -10, 5, -5, 0])
    a = np.random.permutation(np.resize(levels, k // 512 * 4)).reshape(k // 512, 4)
    idx = np.arange(k)
    return np.exp2(a[idx // 512, idx % 128 // 32])


BF16 = ml_dtypes.bfloat16


def bf(x):
    return np.asarray(x, np.float32).astype(BF16)


def f64(x):
    return np.asarray(x).astype(np.float64)


E2M1 = np.array([0.0, 0.5, 1.0, 1.5, 2.0, 3.0, 4.0, 6.0, -0.0, -0.5, -1.0, -1.5, -2.0, -3.0, -4.0, -6.0])


def pack_weight(w, fmt):
    k, n = w.shape
    w = f64(bf(w)).reshape(k // 32, 32, n)
    amax = np.abs(w).max(1)
    if fmt == "e4m3":
        byte = np.frexp(amax)[1] - 1 + 127 - 7
    else:
        mant, ex = np.frexp(amax / 6.0)
        byte = np.where(mant > 0.5, ex, ex - 1) + 127
    byte = np.clip(np.where(amax > 0, byte, 1), 1, 254)
    scaled = (w * np.exp2(127.0 - byte)[:, None, :]).reshape(k, n).astype(np.float32)
    by_word = np.ascontiguousarray(scaled.reshape(k // 512, 128, 4, n).transpose(0, 1, 3, 2))
    if fmt == "e4m3":
        words = by_word.astype(ml_dtypes.float8_e4m3fn).view(np.uint8)
    else:
        c = by_word.astype(ml_dtypes.float4_e2m1fn).view(np.uint8) & 0xF
        words = c[..., 0::2] | (c[..., 1::2] << 4)
    return np.ascontiguousarray(words), np.ascontiguousarray(byte.astype(np.uint8).reshape(k // 512, 16, n))


def unpack_weight(words, scales, fmt):
    g, p, n, _ = words.shape
    if fmt == "e4m3":
        vals = np.ascontiguousarray(words).view(ml_dtypes.float8_e4m3fn).astype(np.float64)
    else:
        nib = np.empty((g, p, n, 4), np.uint8)
        nib[..., 0::2] = words & 0xF
        nib[..., 1::2] = words >> 4
        vals = E2M1[nib]
    vals = vals * np.repeat(np.exp2(scales.astype(np.float64) - 127.0), 8, axis=1)[..., None]
    return vals.transpose(0, 1, 3, 2).reshape(g * 512, n)

def pack4(w):
    words, scales = pack_weight(w, "e2m1")
    return words.reshape(words.shape[0], 128, -1), scales


def unpack4(words, scales):
    return unpack_weight(words.reshape(words.shape[0], 128, -1, 2), scales, "e2m1")


B, X_DIM, Z_DIM, K, H = 12288, 256, 64, 512, 512


def elu(v):
    return np.where(v > 0.0, v, np.exp(np.minimum(v, 0.0)) - 1.0)


def softplus(v):
    return np.maximum(v, 0.0) + np.log(1.0 + np.exp(-np.abs(v)))


def setup_inputs():
    s = mx_kscale(H)
    dec_h1 = bf(elu(np.random.standard_normal((B, H))) * s)
    x = bf(np.random.random((B, X_DIM)))
    dw2_words, dw2_scales = pack4(np.random.standard_normal((H, H)) * 1.25 / np.sqrt(H) / s[:, None])
    db2 = bf(np.random.standard_normal(H) * 0.5)
    dw3_words, dw3_scales = pack4(np.random.standard_normal((H, X_DIM)) * 2.5 / np.sqrt(H))
    db3 = bf(np.random.standard_normal(X_DIM) * 0.8)
    return {"dec_h1": dec_h1,
            "x": x,
            "dw2_words": dw2_words,
            "dw2_scales": dw2_scales,
            "db2": db2,
            "dw3_words": dw3_words,
            "dw3_scales": dw3_scales,
            "db3": db3}


def reference(dec_h1, x, dw2_words, dw2_scales, db2, dw3_words, dw3_scales, db3):
    d2 = elu((mxq(f64(dec_h1), 1, "e4m3") @ unpack4(dw2_words, dw2_scales)) + f64(db2))
    logits = (mxq(d2, 1, "e4m3") @ unpack4(dw3_words, dw3_scales)) + f64(db3)
    return np.sum(f64(x) * logits - softplus(logits), axis=-1)

@@ -1,0 +1,294 @@
+from contextlib import ExitStack
+
+import concourse.mybir as mybir
+from concourse.masks import make_identity
+
+F32 = mybir.dt.float32
+BF16 = mybir.dt.bfloat16
+I32 = mybir.dt.int32
+U32 = mybir.dt.uint32
+U8 = mybir.dt.uint8
+FP8X4 = mybir.dt.float8_e4m3fn_x4
+FP4X4 = mybir.dt.float4_e2m1fn_x4
+ALU = mybir.AluOpType
+ACT = mybir.ActivationFunctionType
+
+P = 128
+PACK = 4
+B, H, X_DIM = 12288, 512, 256
+N_TILES = B // P
+PAIR = 2
+N_PAIRS = N_TILES // PAIR
+CHUNK = 8
+CHUNK_PAIRS = CHUNK // PAIR
+N_CHUNKS = N_TILES // CHUNK
+DEC_BUFS = 3
+N_BLOCKS = 2
+BLOCK_PAIRS = N_PAIRS // N_BLOCKS
+BLOCK_TILES = BLOCK_PAIRS * PAIR
+WORDS = H // 2
+
+FLOPS = 2 * B * H * (H + X_DIM)
+
+
+def tile_gmvae_pb_t_kernel(
+    tc, dec_h1, x, dw2_words, dw2_scales, db2, dw3_words, dw3_scales, db3, out
+):
+    nc = tc.nc
+    dec_rows = dec_h1.rearrange("(p n) k -> p n k", n=N_TILES)
+    x_rows = x.rearrange("(p n) j -> p n j", n=N_TILES)
+    out_rows = out.rearrange("(p n) -> p n", n=N_TILES)
+
+    with ExitStack() as stack:
+        const = stack.enter_context(tc.tile_pool(name="const", bufs=1))
+        dec_pool = stack.enter_context(tc.tile_pool(name="dec", bufs=DEC_BUFS))
+        x_pool = stack.enter_context(tc.tile_pool(name="x", bufs=1))
+        two = stack.enter_context(tc.tile_pool(name="two", bufs=2))
+        four = stack.enter_context(tc.tile_pool(name="four", bufs=2 * PAIR))
+        logit_pool = stack.enter_context(tc.tile_pool(name="logit", bufs=BLOCK_PAIRS + 2))
+        exp_pool = stack.enter_context(tc.tile_pool(name="expl", bufs=BLOCK_PAIRS))
+        ps_dec = stack.enter_context(tc.psum_pool(name="ps_dec", bufs=1))
+        ps_h = stack.enter_context(tc.psum_pool(name="ps_h", bufs=PAIR))
+        ps_v = stack.enter_context(tc.psum_pool(name="ps_v", bufs=2 * PAIR))
+        ps_l = stack.enter_context(tc.psum_pool(name="ps_l", bufs=1))
+        stack.enter_context(tc.manual_schedule())
+
+        ident = const.tile([P, P], F32, name="ident")
+        make_identity(nc, ident[:])
+
+        w2_scales = const.tile([P, H], U8, name="w2_scales", align_bytes=64)
+        w3_scales = const.tile([P, X_DIM], U8, name="w3_scales", align_bytes=64)
+        nc.vector.memset(w2_scales[:].bitcast(I32), 0)
+        nc.vector.memset(w3_scales[:].bitcast(I32), 0)
+        ones = const.tile([P, 1], F32, name="ones")
+        nc.vector.memset(ones[:], 1.0)
+
+        dec_tiles = {}
+
+        def load_dec(chunk):
+            dec_c = dec_pool.tile([P, CHUNK, H], BF16, name="dec_c", tag="dec_c")
+            nc.sync.dma_start(out=dec_c[:], in_=dec_rows[:, chunk * CHUNK : (chunk + 1) * CHUNK, :])
+            dec_tiles[chunk] = dec_c
+
+        x_tiles = {}
+
+        def load_x(block):
+            x_b = x_pool.tile([P, BLOCK_TILES, X_DIM], BF16, name="x_b", tag="x_b")
+            nc.sync.dma_start(
+                out=x_b[:], in_=x_rows[:, block * BLOCK_TILES : (block + 1) * BLOCK_TILES, :]
+            )
+            x_tiles[block] = x_b
+
+        def load_weight(words_dram, scales_dram, scales_sb, n_cols, name):
+            words_sb = const.tile([P, 2 * n_cols], U8, name=name, align_bytes=64)
+            nc.sync.dma_start(out=words_sb[:].bitcast(I32), in_=words_dram[0].bitcast(I32))
+            for q in range(4):
+                nc.sync.dma_start(
+                    out=scales_sb[32 * q : 32 * q + 4, :].bitcast(I32),
+                    in_=scales_dram[0, 4 * q : 4 * q + 4, :].bitcast(I32),
+                )
+            return words_sb
+
+        load_dec(0)
+        w2_words = load_weight(dw2_words, dw2_scales, w2_scales, H, "w2_words")
+        w3_words = load_weight(dw3_words, dw3_scales, w3_scales, X_DIM, "w3_words")
+        for chunk in range(1, DEC_BUFS):
+            load_dec(chunk)
+        load_x(0)
+
+        b2_raw = const.tile([P, H], BF16, name="b2_raw")
+        b3_raw = const.tile([P, X_DIM], BF16, name="b3_raw")
+        nc.scalar.dma_start(out=b2_raw[:], in_=db2.partition_broadcast(P))
+        nc.scalar.dma_start(out=b3_raw[:], in_=db3.partition_broadcast(P))
+        b2_sorted = const.tile([P, PACK, P], F32, name="b2_sorted")
+        nc.vector.tensor_copy(out=b2_sorted[:], in_=b2_raw[:].rearrange("b (p t) -> b t p", t=PACK))
+        b3_pair = const.tile([P, PAIR, X_DIM], F32, name="b3_pair")
+        for r in range(PAIR):
+            nc.vector.tensor_copy(out=b3_pair[:, r, :], in_=b3_raw[:])
+
+        sum_xl = const.tile([P, N_TILES], F32, name="sum_xl")
+        sum_abs = const.tile([P, N_TILES], F32, name="sum_abs")
+        sum_log = const.tile([P, N_TILES], F32, name="sum_log")
+
+        live = {}
+
+        def transpose_dec(pair):
+            words = dec_tiles[pair // CHUNK_PAIRS][:].bitcast(F32)
+            dec_t = ps_dec.tile([P, PAIR, 2, P], F32, name="dec_t", tag="dec_t")
+            for r in range(PAIR):
+                n = (pair % CHUNK_PAIRS) * PAIR + r
+                for u in range(2):
+                    nc.tensor.transpose(dec_t[:, r, u, :], words[:, n, u:WORDS:2], ident[:])
+            live["dec_t", pair] = dec_t
+
+        def regroup_dec(pair):
+            dec_g = two.tile([P, PAIR * P * PACK], BF16, name="dec_g", tag="dec_g", align_bytes=64)
+            nc.scalar.copy(
+                out=dec_g[:].bitcast(F32).rearrange("p (r b u) -> p r b u", r=PAIR, u=2),
+                in_=live["dec_t", pair][:].rearrange("p r u b -> p r b u"),
+            )
+            live["dec_g", pair] = dec_g
+
+        def quantise(grouped, name):
+            codes = two.tile([P, PAIR * P], U32, name=name + "_q", tag=name + "_q", align_bytes=64)
+            scales = two.tile([P, PAIR * P], U8, name=name + "_s", tag=name + "_s", align_bytes=64)
+            nc.vector.quantize_mx(out=codes[:].bitcast(FP8X4), scales=scales[:], in_=grouped[:])
+            return codes, scales
+
+        def quantise_dec(pair):
+            live["dec_q", pair] = quantise(live["dec_g", pair], "dec")
+
+        def first_product(pair):
+            codes, scales = live["dec_q", pair]
+            for r in range(PAIR):
+                rows = slice(r * P, (r + 1) * P)
+                h_acc = ps_h.tile([P, H], F32, name="h_acc", tag="h_acc")
+                nc.tensor.matmul_mx(
+                    out=h_acc[:],
+                    lhsT=codes[:, rows].bitcast(FP8X4),
+                    lhsT_scale=scales[:, rows],
+                    rhs=w2_words[:].bitcast(FP4X4),
+                    rhs_scale=w2_scales[:],
+                    start=True,
+                    stop=True,
+                )
+                live["h_acc", pair, r] = h_acc
+
+        def bias_and_transpose(pair):
+            for r in range(PAIR):
+                v_rows = four.tile([P, PACK, P], F32, name="v_rows", tag="v_rows")
+                nc.vector.tensor_tensor(
+                    out=v_rows[:],
+                    in0=live["h_acc", pair, r][:].rearrange("b (p t) -> b t p", t=PACK),
+                    in1=b2_sorted[:],
+                    op=ALU.add,
+                )
+                v_t = ps_v.tile([P, PACK, P], F32, name="v_t", tag="v_t")
+                for t in range(PACK):
+                    nc.tensor.transpose(v_t[:, t, :], v_rows[:, t, :], ident[:])
+                live["v_t", pair, r] = v_t
+
+        def elu_exp(pair):
+            for r in range(PAIR):
+                exp_v = four.tile([P, PACK, P], F32, name="exp_v", tag="exp_v")
+                nc.scalar.activation(out=exp_v[:], in_=live["v_t", pair, r][:], func=ACT.Exp)
+                expm1 = four.tile([P, P, PACK], F32, name="expm1", tag="expm1")
+                nc.gpsimd.tensor_scalar(
+                    out=expm1[:],
+                    in0=exp_v[:].rearrange("p t b -> p b t"),
+                    scalar1=1.0,
+                    scalar2=-1.0,
+                    op0=ALU.mult,
+                    op1=ALU.add,
+                )
+                live["expm1", pair, r] = expm1
+
+        def elu_and_quantise(pair):
+            d2_g = two.tile([P, PAIR, P, PACK], BF16, name="d2_g", tag="d2_g", align_bytes=64)
+            for r in range(PAIR):
+                nc.vector.scalar_tensor_tensor(
+                    out=d2_g[:, r, :, :],
+                    in0=live["v_t", pair, r][:].rearrange("p t b -> p b t"),
+                    scalar=0.0,
+                    in1=live["expm1", pair, r][:],
+                    op0=ALU.max,
+                    op1=ALU.min,
+                )
+            live["d2_q", pair] = quantise(d2_g[:].rearrange("p r b t -> p (r b t)"), "d2")
+
+        def second_product(pair):
+            codes, scales = live["d2_q", pair]
+            l_acc = ps_l.tile([P, PAIR, X_DIM], F32, name="l_acc", tag="l_acc")
+            for r in range(PAIR):
+                rows = slice(r * P, (r + 1) * P)
+                nc.tensor.matmul_mx(
+                    out=l_acc[:, r, :],
+                    lhsT=codes[:, rows].bitcast(FP8X4),
+                    lhsT_scale=scales[:, rows],
+                    rhs=w3_words[:].bitcast(FP4X4),
+                    rhs_scale=w3_scales[:],
+                    start=True,
+                    stop=True,
+                )
+            live["l_acc", pair] = l_acc
+
+        def logits(pair):
+            logit = logit_pool.tile([P, PAIR, X_DIM], F32, name="logit", tag="logit")
+            nc.vector.tensor_tensor(
+                out=logit[:], in0=live["l_acc", pair][:], in1=b3_pair[:], op=ALU.add
+            )
+            live["logit", pair] = logit
+
+        def abs_logits(pair):
+            abs_l = two.tile([P, PAIR, X_DIM], F32, name="abs_l", tag="abs_l")
+            for r in range(PAIR):
+                n = pair * PAIR + r
+                nc.scalar.activation(
+                    out=abs_l[:, r, :],
+                    in_=live["logit", pair][:, r, :],
+                    func=ACT.Abs,
+                    accum_out=sum_abs[:, n : n + 1],
+                )
+            live["abs_l", pair] = abs_l
+
+        def exp_logits(pair):
+            exp_l = exp_pool.tile([P, PAIR, X_DIM], F32, name="exp_l", tag="exp_l")
+            nc.scalar.activation(out=exp_l[:], in_=live["abs_l", pair][:], func=ACT.Exp, scale=-1.0)
+            live["exp_l", pair] = exp_l
+
+        def logs_and_products(block):
+            for pair in range(block * BLOCK_PAIRS, (block + 1) * BLOCK_PAIRS):
+                for r in range(PAIR):
+                    n = pair * PAIR + r
+                    log_l = two.tile([P, X_DIM], F32, name="log_l", tag="log_l")
+                    nc.scalar.activation(
+                        out=log_l[:],
+                        in_=live["exp_l", pair][:, r, :],
+                        func=ACT.Ln,
+                        bias=ones[:],
+                        accum_out=sum_log[:, n : n + 1],
+                    )
+                    x_l = two.tile([P, X_DIM], F32, name="x_l", tag="x_l")
+                    nc.vector.scalar_tensor_tensor(
+                        out=x_l[:],
+                        in0=x_tiles[block][:, n - block * BLOCK_TILES, :],
+                        scalar=0.5,
+                        in1=live["logit", pair][:, r, :],
+                        op0=ALU.subtract,
+                        op1=ALU.mult,
+                        accum_out=sum_xl[:, n : n + 1],
+                    )
+
+        def run(stage, pair):
+            if 0 <= pair < N_PAIRS:
+                stage(pair)
+
+        for s in range(-3, N_PAIRS + 2):
+            run(bias_and_transpose, s + 1)
+            run(abs_logits, s - 2)
+            run(regroup_dec, s + 2)
+            run(transpose_dec, s + 3)
+            last_of_chunk = (s + 3) % CHUNK_PAIRS == CHUNK_PAIRS - 1
+            next_chunk = (s + 3) // CHUNK_PAIRS + DEC_BUFS
+            if s + 3 >= 0 and last_of_chunk and next_chunk < N_CHUNKS:
+                load_dec(next_chunk)
+            run(elu_exp, s + 1)
+            run(logits, s - 1)
+            run(quantise_dec, s + 2)
+            run(first_product, s + 2)
+            run(exp_logits, s - 2)
+            run(elu_and_quantise, s)
+            run(second_product, s)
+            if s - 2 >= 0 and (s - 2) % BLOCK_PAIRS == BLOCK_PAIRS - 1:
+                block = (s - 2) // BLOCK_PAIRS
+                logs_and_products(block)
+                if block + 1 < N_BLOCKS:
+                    load_x(block + 1)
+
+        partial = const.tile([P, N_TILES], F32, name="partial")
+        nc.vector.scalar_tensor_tensor(
+            out=partial[:], in0=sum_abs[:], scalar=-0.5, in1=sum_xl[:], op0=ALU.mult, op1=ALU.add
+        )
+        result = const.tile([P, N_TILES], F32, name="result")
+        nc.vector.tensor_tensor(out=result[:], in0=partial[:], in1=sum_log[:], op=ALU.subtract)
+        nc.sync.dma_start(out=out_rows, in_=result[:])

@@ -65,10 +65,18 @@ def tile_gmvae_pb_t_kernel(
 
         dec_tiles = {}
 
+        def new_dec_tile(chunk):
+            dec_tiles[chunk] = dec_pool.tile([P, CHUNK, H], BF16, name="dec_c", tag="dec_c")
+
+        def load_dec_tiles(chunk, first, count):
+            n = chunk * CHUNK + first
+            nc.sync.dma_start(
+                out=dec_tiles[chunk][:, first : first + count, :], in_=dec_rows[:, n : n + count, :]
+            )
+
         def load_dec(chunk):
-            dec_c = dec_pool.tile([P, CHUNK, H], BF16, name="dec_c", tag="dec_c")
-            nc.sync.dma_start(out=dec_c[:], in_=dec_rows[:, chunk * CHUNK : (chunk + 1) * CHUNK, :])
-            dec_tiles[chunk] = dec_c
+            new_dec_tile(chunk)
+            load_dec_tiles(chunk, 0, CHUNK)
 
         x_tiles = {}
 
@@ -89,8 +97,11 @@ def tile_gmvae_pb_t_kernel(
                 )
             return words_sb
 
-        load_dec(0)
+        new_dec_tile(0)
+        load_dec_tiles(0, 0, PAIR)
         w2_words = load_weight(dw2_words, dw2_scales, w2_scales, H, "w2_words")
+        for pair in range(1, CHUNK_PAIRS):
+            load_dec_tiles(0, pair * PAIR, PAIR)
         w3_words = load_weight(dw3_words, dw3_scales, w3_scales, X_DIM, "w3_words")
         for chunk in range(1, DEC_BUFS):
             load_dec(chunk)
@@ -183,7 +194,7 @@ def tile_gmvae_pb_t_kernel(
                 )
                 live["expm1", pair, r] = expm1
 
-        def elu_and_quantise(pair):
+        def elu(pair):
             d2_g = two.tile([P, PAIR, P, PACK], BF16, name="d2_g", tag="d2_g", align_bytes=64)
             for r in range(PAIR):
                 nc.vector.scalar_tensor_tensor(
@@ -194,6 +205,10 @@ def tile_gmvae_pb_t_kernel(
                     op0=ALU.max,
                     op1=ALU.min,
                 )
+            live["d2_g", pair] = d2_g
+
+        def quantise_d2(pair):
+            d2_g = live["d2_g", pair]
             live["d2_q", pair] = quantise(d2_g[:].rearrange("p r b t -> p (r b t)"), "d2")
 
         def second_product(pair):
@@ -263,21 +278,22 @@ def tile_gmvae_pb_t_kernel(
             if 0 <= pair < N_PAIRS:
                 stage(pair)
 
-        for s in range(-3, N_PAIRS + 2):
+        for s in range(-4, N_PAIRS + 2):
             run(bias_and_transpose, s + 1)
-            run(abs_logits, s - 2)
-            run(regroup_dec, s + 2)
-            run(transpose_dec, s + 3)
-            last_of_chunk = (s + 3) % CHUNK_PAIRS == CHUNK_PAIRS - 1
-            next_chunk = (s + 3) // CHUNK_PAIRS + DEC_BUFS
-            if s + 3 >= 0 and last_of_chunk and next_chunk < N_CHUNKS:
+            run(first_product, s + 2)
+            run(regroup_dec, s + 3)
+            run(transpose_dec, s + 4)
+            last_of_chunk = (s + 4) % CHUNK_PAIRS == CHUNK_PAIRS - 1
+            next_chunk = (s + 4) // CHUNK_PAIRS + DEC_BUFS
+            if s + 4 >= 0 and last_of_chunk and next_chunk < N_CHUNKS:
                 load_dec(next_chunk)
+            run(abs_logits, s - 2)
             run(elu_exp, s + 1)
             run(logits, s - 1)
-            run(quantise_dec, s + 2)
-            run(first_product, s + 2)
             run(exp_logits, s - 2)
-            run(elu_and_quantise, s)
+            run(elu, s)
+            run(quantise_dec, s + 3)
+            run(quantise_d2, s)
             run(second_product, s)
             if s - 2 >= 0 and (s - 2) % BLOCK_PAIRS == BLOCK_PAIRS - 1:
                 block = (s - 2) // BLOCK_PAIRS

@@ -167,16 +167,32 @@ def tile_gmvae_pb_t_kernel(
 
         def bias_and_transpose(pair):
             for r in range(PAIR):
+                sums = live["h_acc", pair, r][:].rearrange("b (p t) -> b t p", t=PACK)
                 v_rows = four.tile([P, PACK, P], F32, name="v_rows", tag="v_rows")
-                nc.vector.tensor_tensor(
-                    out=v_rows[:],
-                    in0=live["h_acc", pair, r][:].rearrange("b (p t) -> b t p", t=PACK),
-                    in1=b2_sorted[:],
-                    op=ALU.add,
-                )
                 v_t = ps_v.tile([P, PACK, P], F32, name="v_t", tag="v_t")
-                for t in range(PACK):
-                    nc.tensor.transpose(v_t[:, t, :], v_rows[:, t, :], ident[:])
+                if r == 0:
+                    nc.scalar.copy(out=v_rows[:], in_=sums)
+                    for t in range(PACK):
+                        nc.tensor.matmul(
+                            out=v_t[:, t, :],
+                            lhsT=v_rows[:, t, :],
+                            rhs=ident[:],
+                            is_transpose=True,
+                            start=True,
+                            stop=False,
+                        )
+                        nc.tensor.matmul(
+                            out=v_t[:, t, :],
+                            lhsT=b2_sorted[:, t, :],
+                            rhs=ident[:],
+                            is_transpose=True,
+                            start=False,
+                            stop=True,
+                        )
+                else:
+                    nc.vector.tensor_tensor(out=v_rows[:], in0=sums, in1=b2_sorted[:], op=ALU.add)
+                    for t in range(PACK):
+                        nc.tensor.transpose(v_t[:, t, :], v_rows[:, t, :], ident[:])
                 live["v_t", pair, r] = v_t
 
         def elu_exp(pair):

@@ -27,6 +27,7 @@ N_BLOCKS = 2
 BLOCK_PAIRS = N_PAIRS // N_BLOCKS
 BLOCK_TILES = BLOCK_PAIRS * PAIR
 WORDS = H // 2
+SCALAR_EVERY = 3
 
 FLOPS = 2 * B * H * (H + X_DIM)
 
@@ -170,7 +171,7 @@ def tile_gmvae_pb_t_kernel(
                 sums = live["h_acc", pair, r][:].rearrange("b (p t) -> b t p", t=PACK)
                 v_rows = four.tile([P, PACK, P], F32, name="v_rows", tag="v_rows")
                 v_t = ps_v.tile([P, PACK, P], F32, name="v_t", tag="v_t")
-                if r == 0:
+                if (pair * PAIR + r) % SCALAR_EVERY == 0:
                     nc.scalar.copy(out=v_rows[:], in_=sums)
                     for t in range(PACK):
                         nc.tensor.matmul(

@@ -17,17 +17,17 @@ P = 128
 PACK = 4
 B, H, X_DIM = 12288, 512, 256
 N_TILES = B // P
-PAIR = 2
-N_PAIRS = N_TILES // PAIR
-CHUNK = 8
-CHUNK_PAIRS = CHUNK // PAIR
-N_CHUNKS = N_TILES // CHUNK
-DEC_BUFS = 3
+GROUP = 4
+ROWS = GROUP * P
+N_GROUPS = N_TILES // GROUP
+HALF = 2
+DEC_BUFS = 4
 N_BLOCKS = 2
-BLOCK_PAIRS = N_PAIRS // N_BLOCKS
-BLOCK_TILES = BLOCK_PAIRS * PAIR
+BLOCK_GROUPS = N_GROUPS // N_BLOCKS
 WORDS = H // 2
-SCALAR_EVERY = 3
+CLAMP = 40.0
+RELU_ON_VECTOR = ()
+DEC_COPY_ON_VECTOR = (1,)
 
 FLOPS = 2 * B * H * (H + X_DIM)
 
@@ -43,50 +43,49 @@ def tile_gmvae_pb_t_kernel(
     with ExitStack() as stack:
         const = stack.enter_context(tc.tile_pool(name="const", bufs=1))
         dec_pool = stack.enter_context(tc.tile_pool(name="dec", bufs=DEC_BUFS))
-        x_pool = stack.enter_context(tc.tile_pool(name="x", bufs=1))
+        x_pool = stack.enter_context(tc.tile_pool(name="x", bufs=BLOCK_GROUPS + 4))
+        logit_pool = stack.enter_context(tc.tile_pool(name="logit", bufs=BLOCK_GROUPS + 1))
+        exp_pool = stack.enter_context(tc.tile_pool(name="expl", bufs=BLOCK_GROUPS + 1))
         two = stack.enter_context(tc.tile_pool(name="two", bufs=2))
-        four = stack.enter_context(tc.tile_pool(name="four", bufs=2 * PAIR))
-        logit_pool = stack.enter_context(tc.tile_pool(name="logit", bufs=BLOCK_PAIRS + 2))
-        exp_pool = stack.enter_context(tc.tile_pool(name="expl", bufs=BLOCK_PAIRS))
-        ps_dec = stack.enter_context(tc.psum_pool(name="ps_dec", bufs=1))
-        ps_h = stack.enter_context(tc.psum_pool(name="ps_h", bufs=PAIR))
-        ps_v = stack.enter_context(tc.psum_pool(name="ps_v", bufs=2 * PAIR))
-        ps_l = stack.enter_context(tc.psum_pool(name="ps_l", bufs=1))
+        ps_dec = stack.enter_context(tc.psum_pool(name="ps_dec", bufs=GROUP // HALF))
+        ps_h = stack.enter_context(tc.psum_pool(name="ps_h", bufs=PACK))
+        ps_l = stack.enter_context(tc.psum_pool(name="ps_l", bufs=GROUP // HALF))
         stack.enter_context(tc.manual_schedule())
+
+        ones = const.tile([P, 1], F32, name="ones")
+        nc.vector.memset(ones[:], 1.0)
+        warm = const.tile([P, 1], F32, name="warm")
+        nc.scalar.activation(out=warm[:], in_=ones[:], func=ACT.Exp)
 
         ident = const.tile([P, P], F32, name="ident")
         make_identity(nc, ident[:])
 
-        w2_scales = const.tile([P, H], U8, name="w2_scales", align_bytes=64)
+        w2_scales_raw = const.tile([P, H], U8, name="w2_scales_raw", align_bytes=64)
         w3_scales = const.tile([P, X_DIM], U8, name="w3_scales", align_bytes=64)
-        nc.vector.memset(w2_scales[:].bitcast(I32), 0)
+        nc.vector.memset(w2_scales_raw[:].bitcast(I32), 0)
         nc.vector.memset(w3_scales[:].bitcast(I32), 0)
-        ones = const.tile([P, 1], F32, name="ones")
-        nc.vector.memset(ones[:], 1.0)
 
         dec_tiles = {}
 
-        def new_dec_tile(chunk):
-            dec_tiles[chunk] = dec_pool.tile([P, CHUNK, H], BF16, name="dec_c", tag="dec_c")
+        def new_dec_tile(group):
+            dec_tiles[group] = dec_pool.tile([P, GROUP, H], BF16, name="dec_c", tag="dec_c")
 
-        def load_dec_tiles(chunk, first, count):
-            n = chunk * CHUNK + first
+        def load_dec_tiles(group, first, count):
+            n = group * GROUP + first
             nc.sync.dma_start(
-                out=dec_tiles[chunk][:, first : first + count, :], in_=dec_rows[:, n : n + count, :]
+                out=dec_tiles[group][:, first : first + count, :], in_=dec_rows[:, n : n + count, :]
             )
 
-        def load_dec(chunk):
-            new_dec_tile(chunk)
-            load_dec_tiles(chunk, 0, CHUNK)
+        def load_dec(group):
+            new_dec_tile(group)
+            load_dec_tiles(group, 0, GROUP)
 
         x_tiles = {}
 
-        def load_x(block):
-            x_b = x_pool.tile([P, BLOCK_TILES, X_DIM], BF16, name="x_b", tag="x_b")
-            nc.sync.dma_start(
-                out=x_b[:], in_=x_rows[:, block * BLOCK_TILES : (block + 1) * BLOCK_TILES, :]
-            )
-            x_tiles[block] = x_b
+        def load_x(group):
+            x_g = x_pool.tile([P, GROUP, X_DIM], BF16, name="x_g", tag="x_g")
+            nc.sync.dma_start(out=x_g[:], in_=x_rows[:, group * GROUP : (group + 1) * GROUP, :])
+            x_tiles[group] = x_g
 
         def load_weight(words_dram, scales_dram, scales_sb, n_cols, name):
             words_sb = const.tile([P, 2 * n_cols], U8, name=name, align_bytes=64)
@@ -99,183 +98,172 @@ def tile_gmvae_pb_t_kernel(
             return words_sb
 
         new_dec_tile(0)
-        load_dec_tiles(0, 0, PAIR)
-        w2_words = load_weight(dw2_words, dw2_scales, w2_scales, H, "w2_words")
-        for pair in range(1, CHUNK_PAIRS):
-            load_dec_tiles(0, pair * PAIR, PAIR)
+        load_dec_tiles(0, 0, HALF)
+        w2_words_raw = load_weight(dw2_words, dw2_scales, w2_scales_raw, H, "w2_words_raw")
+        load_dec_tiles(0, HALF, HALF)
         w3_words = load_weight(dw3_words, dw3_scales, w3_scales, X_DIM, "w3_words")
-        for chunk in range(1, DEC_BUFS):
-            load_dec(chunk)
-        load_x(0)
+        for group in range(1, DEC_BUFS):
+            load_dec(group)
 
-        b2_raw = const.tile([P, H], BF16, name="b2_raw")
+        b2_raw = const.tile([P, PACK], BF16, name="b2_raw")
+        nc.scalar.dma_start(out=b2_raw[:], in_=db2.rearrange("(p t) -> p t", t=PACK))
+        b2_cols = const.tile([P, PACK], F32, name="b2_cols")
+        nc.vector.tensor_copy(out=b2_cols[:], in_=b2_raw[:])
         b3_raw = const.tile([P, X_DIM], BF16, name="b3_raw")
-        nc.scalar.dma_start(out=b2_raw[:], in_=db2.partition_broadcast(P))
         nc.scalar.dma_start(out=b3_raw[:], in_=db3.partition_broadcast(P))
-        b2_sorted = const.tile([P, PACK, P], F32, name="b2_sorted")
-        nc.vector.tensor_copy(out=b2_sorted[:], in_=b2_raw[:].rearrange("b (p t) -> b t p", t=PACK))
-        b3_pair = const.tile([P, PAIR, X_DIM], F32, name="b3_pair")
-        for r in range(PAIR):
-            nc.vector.tensor_copy(out=b3_pair[:, r, :], in_=b3_raw[:])
+        b3_half = const.tile([P, HALF, X_DIM], F32, name="b3_half")
+        for r in range(HALF):
+            nc.vector.tensor_copy(out=b3_half[:, r, :], in_=b3_raw[:])
+
+        w2_words = const.tile([P, 2 * H], U8, name="w2_words", align_bytes=64)
+        nc.vector.tensor_copy(
+            out=w2_words[:].rearrange("p (t m c) -> p m t c", t=PACK, c=2),
+            in_=w2_words_raw[:].rearrange("p (m t c) -> p m t c", t=PACK, c=2),
+        )
+        w2_scales = const.tile([P, H], U8, name="w2_scales", align_bytes=64)
+        nc.vector.tensor_copy(
+            out=w2_scales[:].rearrange("p (t m) -> p m t", t=PACK),
+            in_=w2_scales_raw[:].rearrange("p (m t) -> p m t", t=PACK),
+        )
 
         sum_xl = const.tile([P, N_TILES], F32, name="sum_xl")
-        sum_abs = const.tile([P, N_TILES], F32, name="sum_abs")
+        sum_c = const.tile([P, N_TILES], F32, name="sum_c")
         sum_log = const.tile([P, N_TILES], F32, name="sum_log")
 
         live = {}
 
-        def transpose_dec(pair):
-            words = dec_tiles[pair // CHUNK_PAIRS][:].bitcast(F32)
-            dec_t = ps_dec.tile([P, PAIR, 2, P], F32, name="dec_t", tag="dec_t")
-            for r in range(PAIR):
-                n = (pair % CHUNK_PAIRS) * PAIR + r
-                for u in range(2):
-                    nc.tensor.transpose(dec_t[:, r, u, :], words[:, n, u:WORDS:2], ident[:])
-            live["dec_t", pair] = dec_t
+        def transpose_dec(group):
+            words = dec_tiles[group][:].bitcast(F32)
+            for half in range(GROUP // HALF):
+                dec_t = ps_dec.tile([P, HALF, 2, P], F32, name="dec_t", tag="dec_t")
+                for r in range(HALF):
+                    for u in range(2):
+                        nc.tensor.transpose(
+                            dec_t[:, r, u, :], words[:, half * HALF + r, u:WORDS:2], ident[:]
+                        )
+                live["dec_t", group, half] = dec_t
 
-        def regroup_dec(pair):
-            dec_g = two.tile([P, PAIR * P * PACK], BF16, name="dec_g", tag="dec_g", align_bytes=64)
-            nc.scalar.copy(
-                out=dec_g[:].bitcast(F32).rearrange("p (r b u) -> p r b u", r=PAIR, u=2),
-                in_=live["dec_t", pair][:].rearrange("p r u b -> p r b u"),
-            )
-            live["dec_g", pair] = dec_g
+        def regroup_dec(group):
+            dec_g = two.tile([P, ROWS * PACK], BF16, name="dec_g", tag="dec_g", align_bytes=64)
+            width = HALF * P * PACK
+            for half in range(GROUP // HALF):
+                dst = dec_g[:, half * width : (half + 1) * width].bitcast(F32)
+                dst = dst.rearrange("p (r b u) -> p r b u", r=HALF, u=2)
+                src = live["dec_t", group, half][:].rearrange("p r u b -> p r b u")
+                if half in DEC_COPY_ON_VECTOR:
+                    nc.vector.tensor_copy(out=dst, in_=src)
+                else:
+                    nc.scalar.copy(out=dst, in_=src)
+            live["dec_g", group] = dec_g
 
         def quantise(grouped, name):
-            codes = two.tile([P, PAIR * P], U32, name=name + "_q", tag=name + "_q", align_bytes=64)
-            scales = two.tile([P, PAIR * P], U8, name=name + "_s", tag=name + "_s", align_bytes=64)
-            nc.vector.quantize_mx(out=codes[:].bitcast(FP8X4), scales=scales[:], in_=grouped[:])
+            codes = two.tile([P, ROWS], U32, name=name + "_q", tag=name + "_q", align_bytes=64)
+            scales = two.tile([P, ROWS], U8, name=name + "_s", tag=name + "_s", align_bytes=64)
+            nc.vector.quantize_mx(out=codes[:].bitcast(FP8X4), scales=scales[:], in_=grouped)
             return codes, scales
 
-        def quantise_dec(pair):
-            live["dec_q", pair] = quantise(live["dec_g", pair], "dec")
+        def quantise_dec(group):
+            live["dec_q", group] = quantise(live["dec_g", group][:], "dec")
 
-        def first_product(pair):
-            codes, scales = live["dec_q", pair]
-            for r in range(PAIR):
-                rows = slice(r * P, (r + 1) * P)
-                h_acc = ps_h.tile([P, H], F32, name="h_acc", tag="h_acc")
-                nc.tensor.matmul_mx(
-                    out=h_acc[:],
-                    lhsT=codes[:, rows].bitcast(FP8X4),
-                    lhsT_scale=scales[:, rows],
-                    rhs=w2_words[:].bitcast(FP4X4),
-                    rhs_scale=w2_scales[:],
-                    start=True,
-                    stop=True,
-                )
-                live["h_acc", pair, r] = h_acc
-
-        def bias_and_transpose(pair):
-            for r in range(PAIR):
-                sums = live["h_acc", pair, r][:].rearrange("b (p t) -> b t p", t=PACK)
-                v_rows = four.tile([P, PACK, P], F32, name="v_rows", tag="v_rows")
-                v_t = ps_v.tile([P, PACK, P], F32, name="v_t", tag="v_t")
-                if (pair * PAIR + r) % SCALAR_EVERY == 0:
-                    nc.scalar.copy(out=v_rows[:], in_=sums)
-                    for t in range(PACK):
-                        nc.tensor.matmul(
-                            out=v_t[:, t, :],
-                            lhsT=v_rows[:, t, :],
-                            rhs=ident[:],
-                            is_transpose=True,
-                            start=True,
-                            stop=False,
-                        )
-                        nc.tensor.matmul(
-                            out=v_t[:, t, :],
-                            lhsT=b2_sorted[:, t, :],
-                            rhs=ident[:],
-                            is_transpose=True,
-                            start=False,
-                            stop=True,
-                        )
-                else:
-                    nc.vector.tensor_tensor(out=v_rows[:], in0=sums, in1=b2_sorted[:], op=ALU.add)
-                    for t in range(PACK):
-                        nc.tensor.transpose(v_t[:, t, :], v_rows[:, t, :], ident[:])
-                live["v_t", pair, r] = v_t
-
-        def elu_exp(pair):
-            for r in range(PAIR):
-                exp_v = four.tile([P, PACK, P], F32, name="exp_v", tag="exp_v")
-                nc.scalar.activation(out=exp_v[:], in_=live["v_t", pair, r][:], func=ACT.Exp)
-                expm1 = four.tile([P, P, PACK], F32, name="expm1", tag="expm1")
-                nc.gpsimd.tensor_scalar(
-                    out=expm1[:],
-                    in0=exp_v[:].rearrange("p t b -> p b t"),
-                    scalar1=1.0,
-                    scalar2=-1.0,
-                    op0=ALU.mult,
-                    op1=ALU.add,
-                )
-                live["expm1", pair, r] = expm1
-
-        def elu(pair):
-            d2_g = two.tile([P, PAIR, P, PACK], BF16, name="d2_g", tag="d2_g", align_bytes=64)
-            for r in range(PAIR):
-                nc.vector.scalar_tensor_tensor(
-                    out=d2_g[:, r, :, :],
-                    in0=live["v_t", pair, r][:].rearrange("p t b -> p b t"),
-                    scalar=0.0,
-                    in1=live["expm1", pair, r][:],
-                    op0=ALU.max,
-                    op1=ALU.min,
-                )
-            live["d2_g", pair] = d2_g
-
-        def quantise_d2(pair):
-            d2_g = live["d2_g", pair]
-            live["d2_q", pair] = quantise(d2_g[:].rearrange("p r b t -> p (r b t)"), "d2")
-
-        def second_product(pair):
-            codes, scales = live["d2_q", pair]
-            l_acc = ps_l.tile([P, PAIR, X_DIM], F32, name="l_acc", tag="l_acc")
-            for r in range(PAIR):
-                rows = slice(r * P, (r + 1) * P)
-                nc.tensor.matmul_mx(
-                    out=l_acc[:, r, :],
-                    lhsT=codes[:, rows].bitcast(FP8X4),
-                    lhsT_scale=scales[:, rows],
-                    rhs=w3_words[:].bitcast(FP4X4),
-                    rhs_scale=w3_scales[:],
-                    start=True,
-                    stop=True,
-                )
-            live["l_acc", pair] = l_acc
-
-        def logits(pair):
-            logit = logit_pool.tile([P, PAIR, X_DIM], F32, name="logit", tag="logit")
-            nc.vector.tensor_tensor(
-                out=logit[:], in0=live["l_acc", pair][:], in1=b3_pair[:], op=ALU.add
+        def first_product(group, t):
+            codes, scales = live["dec_q", group]
+            h_acc = ps_h.tile([P, ROWS], F32, name="h_acc", tag="h_acc")
+            nc.tensor.matmul_mx(
+                out=h_acc[:],
+                lhsT=w2_words[:, 2 * P * t : 2 * P * (t + 1)].bitcast(FP4X4),
+                lhsT_scale=w2_scales[:, P * t : P * (t + 1)],
+                rhs=codes[:].bitcast(FP8X4),
+                rhs_scale=scales[:],
+                start=True,
+                stop=True,
             )
-            live["logit", pair] = logit
+            live["h_acc", group, t] = h_acc
 
-        def abs_logits(pair):
-            abs_l = two.tile([P, PAIR, X_DIM], F32, name="abs_l", tag="abs_l")
-            for r in range(PAIR):
-                n = pair * PAIR + r
-                nc.scalar.activation(
-                    out=abs_l[:, r, :],
-                    in_=live["logit", pair][:, r, :],
-                    func=ACT.Abs,
-                    accum_out=sum_abs[:, n : n + 1],
+        def elu_parts(group, t):
+            if t == 0:
+                live["exp_v", group] = two.tile([P, PACK, ROWS], F32, name="exp_v", tag="exp_v")
+                live["relu_v", group] = two.tile([P, PACK, ROWS], F32, name="relu_v", tag="relu_v")
+            sums = live["h_acc", group, t]
+            bias = b2_cols[:, t : t + 1]
+            nc.scalar.activation(out=live["exp_v", group][:, t, :], in_=sums[:], func=ACT.Exp, bias=bias)
+            relu_v = live["relu_v", group][:, t, :]
+            if t in RELU_ON_VECTOR:
+                nc.vector.tensor_scalar(
+                    out=relu_v, in0=sums[:], scalar1=bias, scalar2=0.0, op0=ALU.add, op1=ALU.max
                 )
-            live["abs_l", pair] = abs_l
+            else:
+                nc.scalar.activation(out=relu_v, in_=sums[:], func=ACT.Relu, bias=bias)
 
-        def exp_logits(pair):
-            exp_l = exp_pool.tile([P, PAIR, X_DIM], F32, name="exp_l", tag="exp_l")
-            nc.scalar.activation(out=exp_l[:], in_=live["abs_l", pair][:], func=ACT.Exp, scale=-1.0)
-            live["exp_l", pair] = exp_l
+        def combine(group):
+            d2_g = two.tile([P, ROWS, PACK], BF16, name="d2_g", tag="d2_g", align_bytes=64)
+            nc.vector.scalar_tensor_tensor(
+                out=d2_g[:],
+                in0=live["exp_v", group][:].rearrange("p t b -> p b t"),
+                scalar=1.0,
+                in1=live["relu_v", group][:].rearrange("p t b -> p b t"),
+                op0=ALU.subtract,
+                op1=ALU.min,
+            )
+            live["d2_g", group] = d2_g
+
+        def quantise_d2(group):
+            live["d2_q", group] = quantise(live["d2_g", group][:].rearrange("p b t -> p (b t)"), "d2")
+
+        def second_product(group):
+            codes, scales = live["d2_q", group]
+            for half in range(GROUP // HALF):
+                l_acc = ps_l.tile([P, HALF, X_DIM], F32, name="l_acc", tag="l_acc")
+                for r in range(HALF):
+                    first = (half * HALF + r) * P
+                    nc.tensor.matmul_mx(
+                        out=l_acc[:, r, :],
+                        lhsT=codes[:, first : first + P].bitcast(FP8X4),
+                        lhsT_scale=scales[:, first : first + P],
+                        rhs=w3_words[:].bitcast(FP4X4),
+                        rhs_scale=w3_scales[:],
+                        start=True,
+                        stop=True,
+                    )
+                live["l_acc", group, half] = l_acc
+
+        def logits(group):
+            logit = logit_pool.tile([P, GROUP, X_DIM], F32, name="logit", tag="logit")
+            for half in range(GROUP // HALF):
+                nc.vector.tensor_tensor(
+                    out=logit[:, half * HALF : (half + 1) * HALF, :],
+                    in0=live["l_acc", group, half][:],
+                    in1=b3_half[:],
+                    op=ALU.add,
+                )
+            live["logit", group] = logit
+
+        def clamp(group):
+            exp_c = exp_pool.tile([P, GROUP, X_DIM], F32, name="exp_c", tag="exp_c")
+            for r in range(GROUP):
+                n = group * GROUP + r
+                nc.vector.tensor_scalar(
+                    out=exp_c[:, r, :],
+                    in0=live["logit", group][:, r, :],
+                    scalar1=CLAMP,
+                    scalar2=None,
+                    op0=ALU.min,
+                    op1=ALU.add,
+                    accum_out=sum_c[:, n : n + 1],
+                )
+            live["exp_c", group] = exp_c
+
+        def exp_logits(group):
+            exp_c = live["exp_c", group]
+            nc.scalar.activation(out=exp_c[:], in_=exp_c[:], func=ACT.Exp)
 
         def logs_and_products(block):
-            for pair in range(block * BLOCK_PAIRS, (block + 1) * BLOCK_PAIRS):
-                for r in range(PAIR):
-                    n = pair * PAIR + r
+            for group in range(block * BLOCK_GROUPS, (block + 1) * BLOCK_GROUPS):
+                for r in range(GROUP):
+                    n = group * GROUP + r
                     log_l = two.tile([P, X_DIM], F32, name="log_l", tag="log_l")
                     nc.scalar.activation(
                         out=log_l[:],
-                        in_=live["exp_l", pair][:, r, :],
+                        in_=live["exp_c", group][:, r, :],
                         func=ACT.Ln,
                         bias=ones[:],
                         accum_out=sum_log[:, n : n + 1],
@@ -283,45 +271,41 @@ def tile_gmvae_pb_t_kernel(
                     x_l = two.tile([P, X_DIM], F32, name="x_l", tag="x_l")
                     nc.vector.scalar_tensor_tensor(
                         out=x_l[:],
-                        in0=x_tiles[block][:, n - block * BLOCK_TILES, :],
-                        scalar=0.5,
-                        in1=live["logit", pair][:, r, :],
+                        in0=x_tiles[group][:, r, :],
+                        scalar=1.0,
+                        in1=live["logit", group][:, r, :],
                         op0=ALU.subtract,
                         op1=ALU.mult,
                         accum_out=sum_xl[:, n : n + 1],
                     )
 
-        def run(stage, pair):
-            if 0 <= pair < N_PAIRS:
-                stage(pair)
+        def run(stage, group):
+            if 0 <= group < N_GROUPS:
+                stage(group)
 
-        for s in range(-4, N_PAIRS + 2):
-            run(bias_and_transpose, s + 1)
-            run(first_product, s + 2)
+        for s in range(-4, N_GROUPS + 4):
+            run(load_x, s + 1)
+            run(combine, s - 1)
+            run(logits, s - 2)
+            run(quantise_d2, s - 1)
+            for t in range(PACK):
+                if 0 <= s < N_GROUPS:
+                    elu_parts(s, t)
+                if 0 <= s + 1 < N_GROUPS:
+                    first_product(s + 1, t)
+            run(second_product, s - 1)
+            run(exp_logits, s - 3)
             run(regroup_dec, s + 3)
             run(transpose_dec, s + 4)
-            last_of_chunk = (s + 4) % CHUNK_PAIRS == CHUNK_PAIRS - 1
-            next_chunk = (s + 4) // CHUNK_PAIRS + DEC_BUFS
-            if s + 4 >= 0 and last_of_chunk and next_chunk < N_CHUNKS:
-                load_dec(next_chunk)
-            run(abs_logits, s - 2)
-            run(elu_exp, s + 1)
-            run(logits, s - 1)
-            run(exp_logits, s - 2)
-            run(elu, s)
-            run(quantise_dec, s + 3)
-            run(quantise_d2, s)
-            run(second_product, s)
-            if s - 2 >= 0 and (s - 2) % BLOCK_PAIRS == BLOCK_PAIRS - 1:
-                block = (s - 2) // BLOCK_PAIRS
-                logs_and_products(block)
-                if block + 1 < N_BLOCKS:
-                    load_x(block + 1)
+            if s + 4 >= 0:
+                run(load_dec, s + 4 + DEC_BUFS)
+            run(clamp, s - 2)
+            run(quantise_dec, s + 2)
+            if s - 3 >= 0 and (s - 3) % BLOCK_GROUPS == BLOCK_GROUPS - 1:
+                logs_and_products((s - 3) // BLOCK_GROUPS)
 
         partial = const.tile([P, N_TILES], F32, name="partial")
-        nc.vector.scalar_tensor_tensor(
-            out=partial[:], in0=sum_abs[:], scalar=-0.5, in1=sum_xl[:], op0=ALU.mult, op1=ALU.add
-        )
+        nc.vector.tensor_tensor(out=partial[:], in0=sum_xl[:], in1=sum_c[:], op=ALU.add)
         result = const.tile([P, N_TILES], F32, name="result")
         nc.vector.tensor_tensor(out=result[:], in0=partial[:], in1=sum_log[:], op=ALU.subtract)
         nc.sync.dma_start(out=out_rows, in_=result[:])

@@ -25,9 +25,6 @@ DEC_BUFS = 4
 N_BLOCKS = 2
 BLOCK_GROUPS = N_GROUPS // N_BLOCKS
 WORDS = H // 2
-CLAMP = 40.0
-RELU_ON_VECTOR = ()
-DEC_COPY_ON_VECTOR = (1,)
 
 FLOPS = 2 * B * H * (H + X_DIM)
 
@@ -45,8 +42,9 @@ def tile_gmvae_pb_t_kernel(
         dec_pool = stack.enter_context(tc.tile_pool(name="dec", bufs=DEC_BUFS))
         x_pool = stack.enter_context(tc.tile_pool(name="x", bufs=BLOCK_GROUPS + 4))
         logit_pool = stack.enter_context(tc.tile_pool(name="logit", bufs=BLOCK_GROUPS + 1))
-        exp_pool = stack.enter_context(tc.tile_pool(name="expl", bufs=BLOCK_GROUPS + 1))
+        exp_pool = stack.enter_context(tc.tile_pool(name="expl", bufs=BLOCK_GROUPS))
         two = stack.enter_context(tc.tile_pool(name="two", bufs=2))
+        one = stack.enter_context(tc.tile_pool(name="one", bufs=1))
         ps_dec = stack.enter_context(tc.psum_pool(name="ps_dec", bufs=GROUP // HALF))
         ps_h = stack.enter_context(tc.psum_pool(name="ps_h", bufs=PACK))
         ps_l = stack.enter_context(tc.psum_pool(name="ps_l", bufs=GROUP // HALF))
@@ -127,7 +125,7 @@ def tile_gmvae_pb_t_kernel(
         )
 
         sum_xl = const.tile([P, N_TILES], F32, name="sum_xl")
-        sum_c = const.tile([P, N_TILES], F32, name="sum_c")
+        sum_abs = const.tile([P, N_TILES], F32, name="sum_abs")
         sum_log = const.tile([P, N_TILES], F32, name="sum_log")
 
         live = {}
@@ -150,10 +148,7 @@ def tile_gmvae_pb_t_kernel(
                 dst = dec_g[:, half * width : (half + 1) * width].bitcast(F32)
                 dst = dst.rearrange("p (r b u) -> p r b u", r=HALF, u=2)
                 src = live["dec_t", group, half][:].rearrange("p r u b -> p r b u")
-                if half in DEC_COPY_ON_VECTOR:
-                    nc.vector.tensor_copy(out=dst, in_=src)
-                else:
-                    nc.scalar.copy(out=dst, in_=src)
+                nc.scalar.copy(out=dst, in_=src)
             live["dec_g", group] = dec_g
 
         def quantise(grouped, name):
@@ -179,30 +174,43 @@ def tile_gmvae_pb_t_kernel(
             )
             live["h_acc", group, t] = h_acc
 
-        def elu_parts(group, t):
+        def exp_v(group, t):
             if t == 0:
                 live["exp_v", group] = two.tile([P, PACK, ROWS], F32, name="exp_v", tag="exp_v")
-                live["relu_v", group] = two.tile([P, PACK, ROWS], F32, name="relu_v", tag="relu_v")
-            sums = live["h_acc", group, t]
-            bias = b2_cols[:, t : t + 1]
-            nc.scalar.activation(out=live["exp_v", group][:, t, :], in_=sums[:], func=ACT.Exp, bias=bias)
-            relu_v = live["relu_v", group][:, t, :]
-            if t in RELU_ON_VECTOR:
-                nc.vector.tensor_scalar(
-                    out=relu_v, in0=sums[:], scalar1=bias, scalar2=0.0, op0=ALU.add, op1=ALU.max
-                )
-            else:
-                nc.scalar.activation(out=relu_v, in_=sums[:], func=ACT.Relu, bias=bias)
+            nc.scalar.activation(
+                out=live["exp_v", group][:, t, :],
+                in_=live["h_acc", group, t][:],
+                func=ACT.Exp,
+                bias=b2_cols[:, t : t + 1],
+            )
 
-        def combine(group):
-            d2_g = two.tile([P, ROWS, PACK], BF16, name="d2_g", tag="d2_g", align_bytes=64)
+        def below_zero(group):
+            exp_all = live["exp_v", group][:].rearrange("p t b -> p (t b)")
+            nc.vector.tensor_scalar(
+                out=exp_all, in0=exp_all, scalar1=-1.0, scalar2=0.0, op0=ALU.add, op1=ALU.min
+            )
+
+        def elu(group, t):
+            if t == 0:
+                live["d2_p", group] = two.tile([P, PACK, ROWS], BF16, name="d2_p", tag="d2_p")
             nc.vector.scalar_tensor_tensor(
+                out=live["d2_p", group][:, t, :],
+                in0=live["h_acc", group, t][:],
+                scalar=b2_cols[:, t : t + 1],
+                in1=live["exp_v", group][:, t, :],
+                op0=ALU.add,
+                op1=ALU.max,
+            )
+
+        def interleave(group):
+            d2_g = one.tile([P, ROWS, PACK], BF16, name="d2_g", tag="d2_g", align_bytes=64)
+            nc.gpsimd.tensor_scalar(
                 out=d2_g[:],
-                in0=live["exp_v", group][:].rearrange("p t b -> p b t"),
-                scalar=1.0,
-                in1=live["relu_v", group][:].rearrange("p t b -> p b t"),
-                op0=ALU.subtract,
-                op1=ALU.min,
+                in0=live["d2_p", group][:].rearrange("p t b -> p b t"),
+                scalar1=1.0,
+                scalar2=0.0,
+                op0=ALU.mult,
+                op1=ALU.add,
             )
             live["d2_g", group] = d2_g
 
@@ -237,24 +245,22 @@ def tile_gmvae_pb_t_kernel(
                 )
             live["logit", group] = logit
 
-        def clamp(group):
-            exp_c = exp_pool.tile([P, GROUP, X_DIM], F32, name="exp_c", tag="exp_c")
+        def abs_logits(group):
+            abs_l = two.tile([P, GROUP, X_DIM], F32, name="abs_l", tag="abs_l")
             for r in range(GROUP):
                 n = group * GROUP + r
-                nc.vector.tensor_scalar(
-                    out=exp_c[:, r, :],
-                    in0=live["logit", group][:, r, :],
-                    scalar1=CLAMP,
-                    scalar2=None,
-                    op0=ALU.min,
-                    op1=ALU.add,
-                    accum_out=sum_c[:, n : n + 1],
+                nc.scalar.activation(
+                    out=abs_l[:, r, :],
+                    in_=live["logit", group][:, r, :],
+                    func=ACT.Abs,
+                    accum_out=sum_abs[:, n : n + 1],
                 )
-            live["exp_c", group] = exp_c
+            live["abs_l", group] = abs_l
 
         def exp_logits(group):
-            exp_c = live["exp_c", group]
-            nc.scalar.activation(out=exp_c[:], in_=exp_c[:], func=ACT.Exp)
+            exp_l = exp_pool.tile([P, GROUP, X_DIM], F32, name="exp_l", tag="exp_l")
+            nc.scalar.activation(out=exp_l[:], in_=live["abs_l", group][:], func=ACT.Exp, scale=-1.0)
+            live["exp_l", group] = exp_l
 
         def logs_and_products(block):
             for group in range(block * BLOCK_GROUPS, (block + 1) * BLOCK_GROUPS):
@@ -263,7 +269,7 @@ def tile_gmvae_pb_t_kernel(
                     log_l = two.tile([P, X_DIM], F32, name="log_l", tag="log_l")
                     nc.scalar.activation(
                         out=log_l[:],
-                        in_=live["exp_c", group][:, r, :],
+                        in_=live["exp_l", group][:, r, :],
                         func=ACT.Ln,
                         bias=ones[:],
                         accum_out=sum_log[:, n : n + 1],
@@ -272,7 +278,7 @@ def tile_gmvae_pb_t_kernel(
                     nc.vector.scalar_tensor_tensor(
                         out=x_l[:],
                         in0=x_tiles[group][:, r, :],
-                        scalar=1.0,
+                        scalar=0.5,
                         in1=live["logit", group][:, r, :],
                         op0=ALU.subtract,
                         op1=ALU.mult,
@@ -285,27 +291,31 @@ def tile_gmvae_pb_t_kernel(
 
         for s in range(-4, N_GROUPS + 4):
             run(load_x, s + 1)
-            run(combine, s - 1)
-            run(logits, s - 2)
-            run(quantise_d2, s - 1)
+            run(quantise_dec, s + 2)
+            run(below_zero, s)
+            run(quantise_d2, s - 2)
+            run(second_product, s - 2)
+            run(interleave, s - 1)
             for t in range(PACK):
                 if 0 <= s < N_GROUPS:
-                    elu_parts(s, t)
+                    elu(s, t)
                 if 0 <= s + 1 < N_GROUPS:
                     first_product(s + 1, t)
-            run(second_product, s - 1)
-            run(exp_logits, s - 3)
-            run(regroup_dec, s + 3)
+                    exp_v(s + 1, t)
+            run(logits, s - 2)
             run(transpose_dec, s + 4)
             if s + 4 >= 0:
                 run(load_dec, s + 4 + DEC_BUFS)
-            run(clamp, s - 2)
-            run(quantise_dec, s + 2)
+            run(abs_logits, s - 3)
+            run(exp_logits, s - 3)
+            run(regroup_dec, s + 4)
             if s - 3 >= 0 and (s - 3) % BLOCK_GROUPS == BLOCK_GROUPS - 1:
                 logs_and_products((s - 3) // BLOCK_GROUPS)
 
         partial = const.tile([P, N_TILES], F32, name="partial")
-        nc.vector.tensor_tensor(out=partial[:], in0=sum_xl[:], in1=sum_c[:], op=ALU.add)
+        nc.vector.scalar_tensor_tensor(
+            out=partial[:], in0=sum_abs[:], scalar=-0.5, in1=sum_xl[:], op0=ALU.mult, op1=ALU.add
+        )
         result = const.tile([P, N_TILES], F32, name="result")
         nc.vector.tensor_tensor(out=result[:], in0=partial[:], in1=sum_log[:], op=ALU.subtract)
         nc.sync.dma_start(out=out_rows, in_=result[:])

@@ -52,6 +52,7 @@ def tile_gmvae_pb_t_kernel(
 
         ones = const.tile([P, 1], F32, name="ones")
         nc.vector.memset(ones[:], 1.0)
+        gate = const.tile([P, 1], F32, name="gate")
         warm = const.tile([P, 1], F32, name="warm")
         nc.scalar.activation(out=warm[:], in_=ones[:], func=ACT.Exp)
 
@@ -186,9 +187,13 @@ def tile_gmvae_pb_t_kernel(
 
         def below_zero(group):
             exp_all = live["exp_v", group][:].rearrange("p t b -> p (t b)")
-            nc.vector.tensor_scalar(
-                out=exp_all, in0=exp_all, scalar1=-1.0, scalar2=0.0, op0=ALU.add, op1=ALU.min
-            )
+            for part in (exp_all[:, : (PACK - 1) * ROWS], exp_all[:, (PACK - 1) * ROWS :]):
+                nc.vector.tensor_scalar(
+                    out=part, in0=part, scalar1=-1.0, scalar2=0.0, op0=ALU.add, op1=ALU.min
+                )
+
+        def open_gate():
+            nc.vector.memset(gate[:], 0.0)
 
         def elu(group, t):
             if t == 0:
@@ -208,7 +213,7 @@ def tile_gmvae_pb_t_kernel(
                 out=d2_g[:],
                 in0=live["d2_p", group][:].rearrange("p t b -> p b t"),
                 scalar1=1.0,
-                scalar2=0.0,
+                scalar2=gate[:],
                 op0=ALU.mult,
                 op1=ALU.add,
             )
@@ -291,10 +296,6 @@ def tile_gmvae_pb_t_kernel(
 
         for s in range(-4, N_GROUPS + 4):
             run(load_x, s + 1)
-            run(quantise_dec, s + 2)
-            run(below_zero, s)
-            run(quantise_d2, s - 2)
-            run(second_product, s - 2)
             run(interleave, s - 1)
             for t in range(PACK):
                 if 0 <= s < N_GROUPS:
@@ -309,8 +310,14 @@ def tile_gmvae_pb_t_kernel(
             run(abs_logits, s - 3)
             run(exp_logits, s - 3)
             run(regroup_dec, s + 4)
+            run(quantise_dec, s + 2)
+            run(quantise_d2, s - 1)
+            run(second_product, s - 1)
             if s - 3 >= 0 and (s - 3) % BLOCK_GROUPS == BLOCK_GROUPS - 1:
                 logs_and_products((s - 3) // BLOCK_GROUPS)
+            run(below_zero, s + 1)
+            if 0 <= s < N_GROUPS:
+                open_gate()
 
         partial = const.tile([P, N_TILES], F32, name="partial")
         nc.vector.scalar_tensor_tensor(

@@ -40,11 +40,10 @@ def tile_gmvae_pb_t_kernel(
     with ExitStack() as stack:
         const = stack.enter_context(tc.tile_pool(name="const", bufs=1))
         dec_pool = stack.enter_context(tc.tile_pool(name="dec", bufs=DEC_BUFS))
-        x_pool = stack.enter_context(tc.tile_pool(name="x", bufs=BLOCK_GROUPS + 4))
-        logit_pool = stack.enter_context(tc.tile_pool(name="logit", bufs=BLOCK_GROUPS + 1))
+        x_pool = stack.enter_context(tc.tile_pool(name="x", bufs=BLOCK_GROUPS + 3))
+        logit_pool = stack.enter_context(tc.tile_pool(name="logit", bufs=BLOCK_GROUPS))
         exp_pool = stack.enter_context(tc.tile_pool(name="expl", bufs=BLOCK_GROUPS))
         two = stack.enter_context(tc.tile_pool(name="two", bufs=2))
-        one = stack.enter_context(tc.tile_pool(name="one", bufs=1))
         ps_dec = stack.enter_context(tc.psum_pool(name="ps_dec", bufs=GROUP // HALF))
         ps_h = stack.enter_context(tc.psum_pool(name="ps_h", bufs=PACK))
         ps_l = stack.enter_context(tc.psum_pool(name="ps_l", bufs=GROUP // HALF))
@@ -185,12 +184,16 @@ def tile_gmvae_pb_t_kernel(
                 bias=b2_cols[:, t : t + 1],
             )
 
-        def below_zero(group):
+        def below_zero_planes(group, first, count):
             exp_all = live["exp_v", group][:].rearrange("p t b -> p (t b)")
-            for part in (exp_all[:, : (PACK - 1) * ROWS], exp_all[:, (PACK - 1) * ROWS :]):
-                nc.vector.tensor_scalar(
-                    out=part, in0=part, scalar1=-1.0, scalar2=0.0, op0=ALU.add, op1=ALU.min
-                )
+            part = exp_all[:, first * ROWS : (first + count) * ROWS]
+            nc.vector.tensor_scalar(
+                out=part, in0=part, scalar1=-1.0, scalar2=0.0, op0=ALU.add, op1=ALU.min
+            )
+
+        def below_zero(group):
+            below_zero_planes(group, 0, PACK - 1)
+            below_zero_planes(group, PACK - 1, 1)
 
         def open_gate():
             nc.vector.memset(gate[:], 0.0)
@@ -208,15 +211,14 @@ def tile_gmvae_pb_t_kernel(
             )
 
         def interleave(group):
-            d2_g = one.tile([P, ROWS, PACK], BF16, name="d2_g", tag="d2_g", align_bytes=64)
-            nc.gpsimd.tensor_scalar(
-                out=d2_g[:],
-                in0=live["d2_p", group][:].rearrange("p t b -> p b t"),
-                scalar1=1.0,
-                scalar2=gate[:],
-                op0=ALU.mult,
-                op1=ALU.add,
-            )
+            d2_g = two.tile([P, ROWS, PACK], BF16, name="d2_g", tag="d2_g", align_bytes=64)
+            planes = live["d2_p", group][:].rearrange("p t b -> p b t")
+            if group < N_GROUPS - 1:
+                nc.gpsimd.tensor_scalar(
+                    out=d2_g[:], in0=planes, scalar1=1.0, scalar2=gate[:], op0=ALU.mult, op1=ALU.add
+                )
+            else:
+                nc.vector.tensor_copy(out=d2_g[:], in_=planes)
             live["d2_g", group] = d2_g
 
         def quantise_d2(group):
@@ -294,29 +296,57 @@ def tile_gmvae_pb_t_kernel(
             if 0 <= group < N_GROUPS:
                 stage(group)
 
-        for s in range(-4, N_GROUPS + 4):
+        def dec_to_sbuf(group):
+            transpose_dec(group)
+            run(load_dec, group + DEC_BUFS)
+            regroup_dec(group)
+
+        def window(s, t):
+            if 0 <= s < N_GROUPS:
+                elu(s, t)
+            if 0 <= s + 1 < N_GROUPS:
+                first_product(s + 1, t)
+                exp_v(s + 1, t)
+
+        for group in range(2):
+            dec_to_sbuf(group)
+            quantise_dec(group)
+        load_x(0)
+        for t in range(PACK):
+            window(-1, t)
+        dec_to_sbuf(2)
+        below_zero_planes(0, 0, 1)
+        for t in range(PACK):
+            if t + 1 < PACK:
+                below_zero_planes(0, t + 1, 1)
+            window(0, t)
+        dec_done = 3
+
+        for s in range(N_GROUPS + 3):
             run(load_x, s + 1)
             run(interleave, s - 1)
-            for t in range(PACK):
-                if 0 <= s < N_GROUPS:
-                    elu(s, t)
-                if 0 <= s + 1 < N_GROUPS:
-                    first_product(s + 1, t)
-                    exp_v(s + 1, t)
+            if s > 0:
+                for t in range(PACK):
+                    window(s, t)
             run(logits, s - 2)
-            run(transpose_dec, s + 4)
-            if s + 4 >= 0:
-                run(load_dec, s + 4 + DEC_BUFS)
-            run(abs_logits, s - 3)
-            run(exp_logits, s - 3)
-            run(regroup_dec, s + 4)
+            if dec_done < min(s + 4, N_GROUPS):
+                dec_to_sbuf(dec_done)
+                dec_done += 1
+            if dec_done < N_GROUPS:
+                transpose_dec(dec_done)
+                run(load_dec, dec_done + DEC_BUFS)
+            run(abs_logits, s - 2)
+            run(exp_logits, s - 2)
+            if dec_done < N_GROUPS:
+                regroup_dec(dec_done)
+                dec_done += 1
             run(quantise_dec, s + 2)
             run(quantise_d2, s - 1)
             run(second_product, s - 1)
-            if s - 3 >= 0 and (s - 3) % BLOCK_GROUPS == BLOCK_GROUPS - 1:
-                logs_and_products((s - 3) // BLOCK_GROUPS)
+            if s - 2 >= 0 and (s - 2) % BLOCK_GROUPS == BLOCK_GROUPS - 1:
+                logs_and_products((s - 2) // BLOCK_GROUPS)
             run(below_zero, s + 1)
-            if 0 <= s < N_GROUPS:
+            if s < N_GROUPS - 1:
                 open_gate()
 
         partial = const.tile([P, N_TILES], F32, name="partial")

@@ -141,14 +141,17 @@ def tile_gmvae_pb_t_kernel(
                         )
                 live["dec_t", group, half] = dec_t
 
-        def regroup_dec(group):
+        def regroup_dec(group, vector_halves=()):
             dec_g = two.tile([P, ROWS * PACK], BF16, name="dec_g", tag="dec_g", align_bytes=64)
             width = HALF * P * PACK
             for half in range(GROUP // HALF):
                 dst = dec_g[:, half * width : (half + 1) * width].bitcast(F32)
                 dst = dst.rearrange("p (r b u) -> p r b u", r=HALF, u=2)
                 src = live["dec_t", group, half][:].rearrange("p r u b -> p r b u")
-                nc.scalar.copy(out=dst, in_=src)
+                if half in vector_halves:
+                    nc.vector.tensor_copy(out=dst, in_=src)
+                else:
+                    nc.scalar.copy(out=dst, in_=src)
             live["dec_g", group] = dec_g
 
         def quantise(grouped, name):
@@ -296,10 +299,10 @@ def tile_gmvae_pb_t_kernel(
             if 0 <= group < N_GROUPS:
                 stage(group)
 
-        def dec_to_sbuf(group):
+        def dec_to_sbuf(group, vector_halves=()):
             transpose_dec(group)
             run(load_dec, group + DEC_BUFS)
-            regroup_dec(group)
+            regroup_dec(group, vector_halves)
 
         def window(s, t):
             if 0 <= s < N_GROUPS:
@@ -309,7 +312,7 @@ def tile_gmvae_pb_t_kernel(
                 exp_v(s + 1, t)
 
         for group in range(2):
-            dec_to_sbuf(group)
+            dec_to_sbuf(group, (1,))
             quantise_dec(group)
         load_x(0)
         for t in range(PACK):
@@ -337,14 +340,18 @@ def tile_gmvae_pb_t_kernel(
                 run(load_dec, dec_done + DEC_BUFS)
             run(abs_logits, s - 2)
             run(exp_logits, s - 2)
-            if dec_done < N_GROUPS:
+            end_of_block = s - 2 >= 0 and (s - 2) % BLOCK_GROUPS == BLOCK_GROUPS - 1
+            if dec_done < N_GROUPS and not end_of_block:
                 regroup_dec(dec_done)
                 dec_done += 1
             run(quantise_dec, s + 2)
             run(quantise_d2, s - 1)
             run(second_product, s - 1)
-            if s - 2 >= 0 and (s - 2) % BLOCK_GROUPS == BLOCK_GROUPS - 1:
+            if end_of_block:
                 logs_and_products((s - 2) // BLOCK_GROUPS)
+                if dec_done < N_GROUPS:
+                    regroup_dec(dec_done, (0, 1))
+                    dec_done += 1
             run(below_zero, s + 1)
             if s < N_GROUPS - 1:
                 open_gate()

from contextlib import ExitStack

import concourse.mybir as mybir
from concourse.masks import make_identity

F32 = mybir.dt.float32
BF16 = mybir.dt.bfloat16
I32 = mybir.dt.int32
U32 = mybir.dt.uint32
U8 = mybir.dt.uint8
FP8X4 = mybir.dt.float8_e4m3fn_x4
FP4X4 = mybir.dt.float4_e2m1fn_x4
ALU = mybir.AluOpType
ACT = mybir.ActivationFunctionType

P = 128
PACK = 4
B, H, X_DIM = 12288, 512, 256
N_TILES = B // P
GROUP = 4
ROWS = GROUP * P
N_GROUPS = N_TILES // GROUP
HALF = 2
DEC_BUFS = 4
N_BLOCKS = 2
BLOCK_GROUPS = N_GROUPS // N_BLOCKS
WORDS = H // 2

FLOPS = 2 * B * H * (H + X_DIM)


def tile_gmvae_pb_t_kernel(
    tc, dec_h1, x, dw2_words, dw2_scales, db2, dw3_words, dw3_scales, db3, out
):
    nc = tc.nc
    dec_rows = dec_h1.rearrange("(p n) k -> p n k", n=N_TILES)
    x_rows = x.rearrange("(p n) j -> p n j", n=N_TILES)
    out_rows = out.rearrange("(p n) -> p n", n=N_TILES)

    with ExitStack() as stack:
        const = stack.enter_context(tc.tile_pool(name="const", bufs=1))
        dec_pool = stack.enter_context(tc.tile_pool(name="dec", bufs=DEC_BUFS))
        x_pool = stack.enter_context(tc.tile_pool(name="x", bufs=BLOCK_GROUPS + 3))
        logit_pool = stack.enter_context(tc.tile_pool(name="logit", bufs=BLOCK_GROUPS))
        exp_pool = stack.enter_context(tc.tile_pool(name="expl", bufs=BLOCK_GROUPS))
        two = stack.enter_context(tc.tile_pool(name="two", bufs=2))
        ps_dec = stack.enter_context(tc.psum_pool(name="ps_dec", bufs=GROUP // HALF))
        ps_h = stack.enter_context(tc.psum_pool(name="ps_h", bufs=PACK))
        ps_l = stack.enter_context(tc.psum_pool(name="ps_l", bufs=GROUP // HALF))
        stack.enter_context(tc.manual_schedule())

        ones = const.tile([P, 1], F32, name="ones")
        nc.vector.memset(ones[:], 1.0)
        gate = const.tile([P, 1], F32, name="gate")
        warm = const.tile([P, 1], F32, name="warm")
        nc.scalar.activation(out=warm[:], in_=ones[:], func=ACT.Exp)

        ident = const.tile([P, P], F32, name="ident")
        make_identity(nc, ident[:])

        w2_scales_raw = const.tile([P, H], U8, name="w2_scales_raw", align_bytes=64)
        w3_scales = const.tile([P, X_DIM], U8, name="w3_scales", align_bytes=64)
        nc.vector.memset(w2_scales_raw[:].bitcast(I32), 0)
        nc.vector.memset(w3_scales[:].bitcast(I32), 0)

        dec_tiles = {}

        def new_dec_tile(group):
            dec_tiles[group] = dec_pool.tile([P, GROUP, H], BF16, name="dec_c", tag="dec_c")

        def load_dec_tiles(group, first, count):
            n = group * GROUP + first
            nc.sync.dma_start(
                out=dec_tiles[group][:, first : first + count, :], in_=dec_rows[:, n : n + count, :]
            )

        def load_dec(group):
            new_dec_tile(group)
            load_dec_tiles(group, 0, GROUP)

        x_tiles = {}

        def load_x(group):
            x_g = x_pool.tile([P, GROUP, X_DIM], BF16, name="x_g", tag="x_g")
            nc.sync.dma_start(out=x_g[:], in_=x_rows[:, group * GROUP : (group + 1) * GROUP, :])
            x_tiles[group] = x_g

        def load_weight(words_dram, scales_dram, scales_sb, n_cols, name):
            words_sb = const.tile([P, 2 * n_cols], U8, name=name, align_bytes=64)
            nc.sync.dma_start(out=words_sb[:].bitcast(I32), in_=words_dram[0].bitcast(I32))
            for q in range(4):
                nc.sync.dma_start(
                    out=scales_sb[32 * q : 32 * q + 4, :].bitcast(I32),
                    in_=scales_dram[0, 4 * q : 4 * q + 4, :].bitcast(I32),
                )
            return words_sb

        new_dec_tile(0)
        load_dec_tiles(0, 0, HALF)
        w2_words_raw = load_weight(dw2_words, dw2_scales, w2_scales_raw, H, "w2_words_raw")
        load_dec_tiles(0, HALF, HALF)
        w3_words = load_weight(dw3_words, dw3_scales, w3_scales, X_DIM, "w3_words")
        for group in range(1, DEC_BUFS):
            load_dec(group)

        b2_raw = const.tile([P, PACK], BF16, name="b2_raw")
        nc.scalar.dma_start(out=b2_raw[:], in_=db2.rearrange("(p t) -> p t", t=PACK))
        b2_cols = const.tile([P, PACK], F32, name="b2_cols")
        nc.vector.tensor_copy(out=b2_cols[:], in_=b2_raw[:])
        b3_raw = const.tile([P, X_DIM], BF16, name="b3_raw")
        nc.scalar.dma_start(out=b3_raw[:], in_=db3.partition_broadcast(P))
        b3_half = const.tile([P, HALF, X_DIM], F32, name="b3_half")
        for r in range(HALF):
            nc.vector.tensor_copy(out=b3_half[:, r, :], in_=b3_raw[:])

        w2_words = const.tile([P, 2 * H], U8, name="w2_words", align_bytes=64)
        nc.vector.tensor_copy(
            out=w2_words[:].rearrange("p (t m c) -> p m t c", t=PACK, c=2),
            in_=w2_words_raw[:].rearrange("p (m t c) -> p m t c", t=PACK, c=2),
        )
        w2_scales = const.tile([P, H], U8, name="w2_scales", align_bytes=64)
        nc.vector.tensor_copy(
            out=w2_scales[:].rearrange("p (t m) -> p m t", t=PACK),
            in_=w2_scales_raw[:].rearrange("p (m t) -> p m t", t=PACK),
        )

        sum_xl = const.tile([P, N_TILES], F32, name="sum_xl")
        sum_abs = const.tile([P, N_TILES], F32, name="sum_abs")
        sum_log = const.tile([P, N_TILES], F32, name="sum_log")

        live = {}

        def transpose_dec(group):
            words = dec_tiles[group][:].bitcast(F32)
            for half in range(GROUP // HALF):
                dec_t = ps_dec.tile([P, HALF, 2, P], F32, name="dec_t", tag="dec_t")
                for r in range(HALF):
                    for u in range(2):
                        nc.tensor.transpose(
                            dec_t[:, r, u, :], words[:, half * HALF + r, u:WORDS:2], ident[:]
                        )
                live["dec_t", group, half] = dec_t

        def regroup_dec(group, vector_halves=()):
            dec_g = two.tile([P, ROWS * PACK], BF16, name="dec_g", tag="dec_g", align_bytes=64)
            width = HALF * P * PACK
            for half in range(GROUP // HALF):
                dst = dec_g[:, half * width : (half + 1) * width].bitcast(F32)
                dst = dst.rearrange("p (r b u) -> p r b u", r=HALF, u=2)
                src = live["dec_t", group, half][:].rearrange("p r u b -> p r b u")
                if half in vector_halves:
                    nc.vector.tensor_copy(out=dst, in_=src)
                else:
                    nc.scalar.copy(out=dst, in_=src)
            live["dec_g", group] = dec_g

        def quantise(grouped, name):
            codes = two.tile([P, ROWS], U32, name=name + "_q", tag=name + "_q", align_bytes=64)
            scales = two.tile([P, ROWS], U8, name=name + "_s", tag=name + "_s", align_bytes=64)
            nc.vector.quantize_mx(out=codes[:].bitcast(FP8X4), scales=scales[:], in_=grouped)
            return codes, scales

        def quantise_dec(group):
            live["dec_q", group] = quantise(live["dec_g", group][:], "dec")

        def first_product(group, t):
            codes, scales = live["dec_q", group]
            h_acc = ps_h.tile([P, ROWS], F32, name="h_acc", tag="h_acc")
            nc.tensor.matmul_mx(
                out=h_acc[:],
                lhsT=w2_words[:, 2 * P * t : 2 * P * (t + 1)].bitcast(FP4X4),
                lhsT_scale=w2_scales[:, P * t : P * (t + 1)],
                rhs=codes[:].bitcast(FP8X4),
                rhs_scale=scales[:],
                start=True,
                stop=True,
            )
            live["h_acc", group, t] = h_acc

        def exp_v(group, t):
            if t == 0:
                live["exp_v", group] = two.tile([P, PACK, ROWS], F32, name="exp_v", tag="exp_v")
            nc.scalar.activation(
                out=live["exp_v", group][:, t, :],
                in_=live["h_acc", group, t][:],
                func=ACT.Exp,
                bias=b2_cols[:, t : t + 1],
            )

        def below_zero_planes(group, first, count):
            exp_all = live["exp_v", group][:].rearrange("p t b -> p (t b)")
            part = exp_all[:, first * ROWS : (first + count) * ROWS]
            nc.vector.tensor_scalar(
                out=part, in0=part, scalar1=-1.0, scalar2=0.0, op0=ALU.add, op1=ALU.min
            )

        def below_zero(group):
            below_zero_planes(group, 0, PACK - 1)
            below_zero_planes(group, PACK - 1, 1)

        def open_gate():
            nc.vector.memset(gate[:], 0.0)

        def elu(group, t):
            if t == 0:
                live["d2_p", group] = two.tile([P, PACK, ROWS], BF16, name="d2_p", tag="d2_p")
            nc.vector.scalar_tensor_tensor(
                out=live["d2_p", group][:, t, :],
                in0=live["h_acc", group, t][:],
                scalar=b2_cols[:, t : t + 1],
                in1=live["exp_v", group][:, t, :],
                op0=ALU.add,
                op1=ALU.max,
            )

        def interleave(group):
            d2_g = two.tile([P, ROWS, PACK], BF16, name="d2_g", tag="d2_g", align_bytes=64)
            planes = live["d2_p", group][:].rearrange("p t b -> p b t")
            if group < N_GROUPS - 1:
                nc.gpsimd.tensor_scalar(
                    out=d2_g[:], in0=planes, scalar1=1.0, scalar2=gate[:], op0=ALU.mult, op1=ALU.add
                )
            else:
                nc.vector.tensor_copy(out=d2_g[:], in_=planes)
            live["d2_g", group] = d2_g

        def quantise_d2(group):
            live["d2_q", group] = quantise(live["d2_g", group][:].rearrange("p b t -> p (b t)"), "d2")

        def second_product(group):
            codes, scales = live["d2_q", group]
            for half in range(GROUP // HALF):
                l_acc = ps_l.tile([P, HALF, X_DIM], F32, name="l_acc", tag="l_acc")
                for r in range(HALF):
                    first = (half * HALF + r) * P
                    nc.tensor.matmul_mx(
                        out=l_acc[:, r, :],
                        lhsT=codes[:, first : first + P].bitcast(FP8X4),
                        lhsT_scale=scales[:, first : first + P],
                        rhs=w3_words[:].bitcast(FP4X4),
                        rhs_scale=w3_scales[:],
                        start=True,
                        stop=True,
                    )
                live["l_acc", group, half] = l_acc

        def logits(group):
            logit = logit_pool.tile([P, GROUP, X_DIM], F32, name="logit", tag="logit")
            for half in range(GROUP // HALF):
                nc.vector.tensor_tensor(
                    out=logit[:, half * HALF : (half + 1) * HALF, :],
                    in0=live["l_acc", group, half][:],
                    in1=b3_half[:],
                    op=ALU.add,
                )
            live["logit", group] = logit

        def abs_logits(group):
            abs_l = two.tile([P, GROUP, X_DIM], F32, name="abs_l", tag="abs_l")
            for r in range(GROUP):
                n = group * GROUP + r
                nc.scalar.activation(
                    out=abs_l[:, r, :],
                    in_=live["logit", group][:, r, :],
                    func=ACT.Abs,
                    accum_out=sum_abs[:, n : n + 1],
                )
            live["abs_l", group] = abs_l

        def exp_logits(group):
            exp_l = exp_pool.tile([P, GROUP, X_DIM], F32, name="exp_l", tag="exp_l")
            nc.scalar.activation(out=exp_l[:], in_=live["abs_l", group][:], func=ACT.Exp, scale=-1.0)
            live["exp_l", group] = exp_l

        def logs_and_products(block):
            for group in range(block * BLOCK_GROUPS, (block + 1) * BLOCK_GROUPS):
                for r in range(GROUP):
                    n = group * GROUP + r
                    log_l = two.tile([P, X_DIM], F32, name="log_l", tag="log_l")
                    nc.scalar.activation(
                        out=log_l[:],
                        in_=live["exp_l", group][:, r, :],
                        func=ACT.Ln,
                        bias=ones[:],
                        accum_out=sum_log[:, n : n + 1],
                    )
                    x_l = two.tile([P, X_DIM], F32, name="x_l", tag="x_l")
                    nc.vector.scalar_tensor_tensor(
                        out=x_l[:],
                        in0=x_tiles[group][:, r, :],
                        scalar=0.5,
                        in1=live["logit", group][:, r, :],
                        op0=ALU.subtract,
                        op1=ALU.mult,
                        accum_out=sum_xl[:, n : n + 1],
                    )

        def run(stage, group):
            if 0 <= group < N_GROUPS:
                stage(group)

        def dec_to_sbuf(group, vector_halves=()):
            transpose_dec(group)
            run(load_dec, group + DEC_BUFS)
            regroup_dec(group, vector_halves)

        def window(s, t):
            if 0 <= s < N_GROUPS:
                elu(s, t)
            if 0 <= s + 1 < N_GROUPS:
                first_product(s + 1, t)
                exp_v(s + 1, t)

        for group in range(2):
            dec_to_sbuf(group, (1,))
            quantise_dec(group)
        load_x(0)
        for t in range(PACK):
            window(-1, t)
        dec_to_sbuf(2)
        below_zero_planes(0, 0, 1)
        for t in range(PACK):
            if t + 1 < PACK:
                below_zero_planes(0, t + 1, 1)
            window(0, t)
        dec_done = 3

        for s in range(N_GROUPS + 3):
            run(load_x, s + 1)
            run(interleave, s - 1)
            if s > 0:
                for t in range(PACK):
                    window(s, t)
            run(logits, s - 2)
            if dec_done < min(s + 4, N_GROUPS):
                dec_to_sbuf(dec_done)
                dec_done += 1
            if dec_done < N_GROUPS:
                transpose_dec(dec_done)
                run(load_dec, dec_done + DEC_BUFS)
            run(abs_logits, s - 2)
            run(exp_logits, s - 2)
            end_of_block = s - 2 >= 0 and (s - 2) % BLOCK_GROUPS == BLOCK_GROUPS - 1
            if dec_done < N_GROUPS and not end_of_block:
                regroup_dec(dec_done)
                dec_done += 1
            run(quantise_dec, s + 2)
            run(quantise_d2, s - 1)
            run(second_product, s - 1)
            if end_of_block:
                logs_and_products((s - 2) // BLOCK_GROUPS)
                if dec_done < N_GROUPS:
                    regroup_dec(dec_done, (0, 1))
                    dec_done += 1
            run(below_zero, s + 1)
            if s < N_GROUPS - 1:
                open_gate()

        partial = const.tile([P, N_TILES], F32, name="partial")
        nc.vector.scalar_tensor_tensor(
            out=partial[:], in0=sum_abs[:], scalar=-0.5, in1=sum_xl[:], op0=ALU.mult, op1=ALU.add
        )
        result = const.tile([P, N_TILES], F32, name="result")
        nc.vector.tensor_tensor(out=result[:], in0=partial[:], in1=sum_log[:], op=ALU.subtract)
        nc.sync.dma_start(out=out_rows, in_=result[:])
